import numpy as np
import ml_dtypes


def mxq(x, axis, fmt="e4m3"):
    dtype, down = {"e4m3": (ml_dtypes.float8_e4m3fn, 7), "e5m2": (ml_dtypes.float8_e5m2, 14)}[fmt]
    v = np.moveaxis(np.asarray(x, np.float32).astype(ml_dtypes.bfloat16).astype(np.float64), axis, -1)
    blocks = v.reshape(v.shape[:-1] + (-1, 32))
    amax = np.abs(blocks).max(-1, keepdims=True)
    byte = np.maximum(np.where(amax > 0, np.frexp(amax)[1] - 1 + 127, 0) - down, 1)
    scale = np.exp2(byte - 127.0)
    codes = (blocks / scale).astype(np.float32).astype(dtype).astype(np.float64)
    return np.moveaxis((codes * scale).reshape(v.shape), -1, axis)


WIDE = False


def mx_kscale(k):
    if not WIDE:
        return np.ones(k)
    levels = np.array([10, -10, 5, -5, 0])
    if k % 512:
        return np.exp2(np.random.permutation(np.resize(levels, k // 32))).repeat(32)
    a = np.empty((k // 512, 16))
    for p in range(k // 512):
        a[p, :8] = np.random.permutation(np.resize(levels, 8))
        for g in range(8):
            far = levels[np.abs(levels - a[p, g]) >= 10]
            a[p, g + 8] = far[np.random.randint(len(far))]
    return np.exp2(a.ravel()).repeat(32)


BF16 = ml_dtypes.bfloat16


def bf(x):
    return np.asarray(x, np.float32).astype(BF16)


def f64(x):
    return np.asarray(x).astype(np.float64)


B, I, O, M = 1024, 512, 256, 2


def modemul(a, c):
    return (a.transpose(2, 3, 4, 0, 1) @ c.transpose(2, 3, 4, 0, 1)).transpose(3, 4, 0, 1, 2)


def setup_inputs():
    s = mx_kscale(I)
    sx = s[None, :, None, None, None]
    sw = s[:, None, None, None, None]
    xs, ws = (B, I, M, M, M), (I, O, M, M, M)
    return {"x_real": bf(np.random.standard_normal(xs) * sx),
            "x_imag": bf(np.random.standard_normal(xs) * sx),
            "w_real": bf(np.random.standard_normal(ws) / np.sqrt(I) / sw),
            "w_imag": bf(np.random.standard_normal(ws) / np.sqrt(I) / sw)}


def reference(x_real, x_imag, w_real, w_imag):
    xr, xi = mxq(f64(x_real), 1, "e4m3"), mxq(f64(x_imag), 1, "e4m3")
    wr, wi = mxq(f64(w_real), 0, "e4m3"), mxq(f64(w_imag), 0, "e4m3")
    re = modemul(xr, wr) - modemul(xi, wi)
    im = modemul(xr, wi) + modemul(xi, wr)
    return np.stack([re, im])

@@ -1,0 +1,240 @@
+from contextlib import ExitStack
+
+import concourse.mybir as mybir
+from concourse.masks import make_identity
+
+F32 = mybir.dt.float32
+BF16 = mybir.dt.bfloat16
+U32 = mybir.dt.uint32
+U8 = mybir.dt.uint8
+FP8X4 = mybir.dt.float8_e4m3fn_x4
+MULT = mybir.AluOpType.mult
+ADD = mybir.AluOpType.add
+
+P = 128
+B, I, O, NM = 1024, 512, 256, 8
+NBT = B // P
+FLOPS = 2 * 4 * NM * B * I * O
+
+
+def tile_mymodel_t_kernel(tc, x_real, x_imag, w_real, w_imag, out):
+    nc = tc.nc
+    xs_dram = [
+        x_real.rearrange("b i x y z -> b (i x y z)"),
+        x_imag.rearrange("b i x y z -> b (i x y z)"),
+    ]
+    w_dram = {
+        "r": w_real.rearrange("(p t) o x y z -> p t (o x y z)", t=4),
+        "i": w_imag.rearrange("(p t) o x y z -> p t (o x y z)", t=4),
+    }
+    out_dram = out.rearrange("c b o x y z -> b c (o x y z)")
+
+    with ExitStack() as ctx:
+        const = ctx.enter_context(tc.tile_pool(name="const", bufs=1))
+        big = ctx.enter_context(tc.tile_pool(name="big", bufs=10))
+        wpool = ctx.enter_context(tc.tile_pool(name="wpool", bufs=1))
+        spool = ctx.enter_context(tc.tile_pool(name="spool", bufs=4))
+        gpool = ctx.enter_context(tc.tile_pool(name="gpool", bufs=2))
+        cpool = ctx.enter_context(tc.tile_pool(name="cpool", bufs=8))
+        opool = ctx.enter_context(tc.tile_pool(name="opool", bufs=3))
+        ps_t = ctx.enter_context(tc.psum_pool(name="ps_t", bufs=4))
+        ps_o = ctx.enter_context(tc.psum_pool(name="ps_o", bufs=4))
+        ctx.enter_context(tc.manual_schedule())
+
+        ident = const.tile([P, P], F32, name="ident")
+        make_identity(nc, ident[:])
+
+        x_tiles = {}
+
+        def load_x(bt):
+            for s in range(2):
+                xt = big.tile([P, I * NM], BF16, name="xt", tag="big")
+                nc.sync.dma_start(out=xt[:], in_=xs_dram[s][bt * P : (bt + 1) * P, :])
+                x_tiles[(bt, s)] = xt
+
+        w_raw = {}
+
+        def load_w(v, oh):
+            wt = big.tile([P, 4, P * NM], BF16, name="wt", tag="big")
+            for u in range(2):
+                nc.sync.dma_start(
+                    out=wt[:, 2 * u : 2 * u + 2, :],
+                    in_=w_dram[v][:, 2 * u : 2 * u + 2, oh * P * NM : (oh + 1) * P * NM],
+                )
+            w_raw[(v, oh)] = wt
+
+        w_codes = {}
+        w_scales = {}
+        for v in ("r", "i", "n"):
+            for oh in range(2):
+                w_codes[(v, oh)] = wpool.tile([P, NM * P], U32, name="wc_%s%d" % (v, oh), align_bytes=64)
+                w_scales[(v, oh)] = wpool.tile([P, NM * P], U8, name="ws_%s%d" % (v, oh), align_bytes=64)
+
+        w_grouped = {}
+
+        def regroup_w(eng, v, oh, h):
+            g = wpool.tile([P, 2048], BF16, name="g_%s%d" % (v, h), align_bytes=64)
+            w_grouped[(v, oh, h)] = g
+            o_ap = g[:].rearrange("p (m o t) -> p o t m", m=4, t=4)
+            i_ap = w_raw[(v, oh)][:].rearrange("p t (o m) -> p o t m", m=NM)[:, :, :, 4 * h : 4 * h + 4]
+            if eng == "v":
+                nc.vector.tensor_copy(out=o_ap, in_=i_ap)
+            elif eng == "s":
+                nc.scalar.copy(out=o_ap, in_=i_ap)
+            else:
+                nc.gpsimd.tensor_scalar(out=o_ap, in0=i_ap, scalar1=1.0, scalar2=0.0, op0=MULT, op1=ADD)
+
+        def quant_w(v, oh, h):
+            cols = slice(h * 512, (h + 1) * 512)
+            nc.vector.quantize_mx(
+                out=w_codes[(v, oh)][:, cols].bitcast(FP8X4),
+                scales=w_scales[(v, oh)][:, cols],
+                in_=w_grouped[(v, oh, h)][:],
+            )
+
+        def quant_w_half(oh, h):
+            quant_w("i", oh, h)
+            gn = wpool.tile([P, 2048], BF16, name="g_n%d" % h, align_bytes=64)
+            w_grouped[("n", oh, h)] = gn
+            nc.vector.tensor_scalar_mul(out=gn[:], in0=w_grouped[("i", oh, h)][:], scalar1=-1.0)
+            quant_w("r", oh, h)
+            quant_w("n", oh, h)
+
+        x_sorted = {}
+
+        def sort_x(u, s):
+            bt, h = u // 2, u % 2
+            xs = spool.tile([P, 4 * I], BF16, name="xs")
+            nc.gpsimd.tensor_scalar(
+                out=xs[:].rearrange("p (m i) -> p i m", m=4),
+                in0=x_tiles[(bt, s)][:].rearrange("p (i m) -> p i m", m=NM)[:, :, 4 * h : 4 * h + 4],
+                scalar1=1.0,
+                scalar2=0.0,
+                op0=MULT,
+                op1=ADD,
+            )
+            x_sorted[(u, s)] = xs
+
+        x_codes = {}
+
+        def tau(u):
+            bt, h = u // 2, u % 2
+            grouped = gpool.tile([P, 4096], BF16, name="grouped", align_bytes=64)
+            banks = []
+            for s in range(2):
+                if (u, s) in x_sorted:
+                    xw = x_sorted[(u, s)][:].bitcast(F32).rearrange("p (m j u) -> p m u j", m=4, u=2)
+                else:
+                    xw = x_tiles[(bt, s)][:].bitcast(F32).rearrange("p (j u e q) -> p u e q j", u=2, e=2, q=4)
+                for mpl in range(2):
+                    tb = ps_t.tile([P, 512], F32, name="tb")
+                    for t in range(4):
+                        if (u, s) in x_sorted:
+                            src = xw[:, 2 * mpl + t // 2, t % 2, :]
+                        else:
+                            src = xw[:, t // 2, t % 2, 2 * h + mpl, :]
+                        nc.tensor.transpose(tb[:, t * P : (t + 1) * P], src, ident[:])
+                    banks.append(tb)
+            for k in range(4):
+                part = grouped[:, k * 1024 : (k + 1) * 1024]
+                if (u, k // 2) in x_sorted:
+                    o_ap = part.bitcast(F32).rearrange("p (m b u) -> p m b u", m=2, u=2)
+                    i_ap = banks[k][:].rearrange("p (m u b) -> p m b u", m=2, u=2)
+                else:
+                    o_ap = part.rearrange("p (m b t) -> p m b t", m=2, t=4)
+                    i_ap = banks[k][:].bitcast(BF16).rearrange("p (t b m) -> p m b t", t=4, m=2)
+                on_vector = (k == 3) if u < 6 else (k % 2 == 1)
+                if on_vector:
+                    nc.vector.tensor_copy(out=o_ap, in_=i_ap)
+                else:
+                    nc.scalar.copy(out=o_ap, in_=i_ap)
+            xc = cpool.tile([P, 1024], U32, name="xc", align_bytes=64)
+            xsc = cpool.tile([P, 1024], U8, name="xsc", align_bytes=64)
+            nc.vector.quantize_mx(out=xc[:].bitcast(FP8X4), scales=xsc[:], in_=grouped[:])
+            x_codes[u] = (xc, xsc)
+
+        def store(ot, bt, oh, c0, c1):
+            nc.sync.dma_start(
+                out=out_dram[bt * P : (bt + 1) * P, c0:c1, oh * P * NM : (oh + 1) * P * NM],
+                in_=ot[:, c0:c1].rearrange("p c o m -> p c (o m)"),
+            )
+
+        def mu(bt, oh, last):
+            ot = opool.tile([P, 2, P, NM], F32, name="ot")
+            order = ((1, 0), (1, 1), (0, 0), (0, 1)) if last else ((1, 0), (0, 0), (1, 1), (0, 1))
+            for n_bank, (c, h) in enumerate(order):
+                xc, xsc = x_codes[2 * bt + h]
+                ob = ps_o.tile([P, 512], F32, name="ob")
+                for ml in range(4):
+                    pairs = ((0, "r"), (1, "n")) if c == 0 else ((0, "i"), (1, "r"))
+                    for n, (s, v) in enumerate(pairs):
+                        sl = slice((4 * s + ml) * P, (4 * s + ml + 1) * P)
+                        wl = slice((4 * h + ml) * P, (4 * h + ml + 1) * P)
+                        nc.tensor.matmul_mx(
+                            out=ob[:, ml * P : (ml + 1) * P],
+                            lhsT=xc[:, sl].bitcast(FP8X4),
+                            lhsT_scale=xsc[:, sl],
+                            rhs=w_codes[(v, oh)][:, wl].bitcast(FP8X4),
+                            rhs_scale=w_scales[(v, oh)][:, wl],
+                            start=(n == 0),
+                            stop=(n == 1),
+                        )
+                o_ap = ot[:, c, :, 4 * h : 4 * h + 4]
+                i_ap = ob[:].rearrange("p (m o) -> p o m", m=4)
+                if c == 0 and oh == 0 and bt >= 2:
+                    nc.vector.tensor_copy(out=o_ap, in_=i_ap)
+                else:
+                    nc.scalar.copy(out=o_ap, in_=i_ap)
+                if last and n_bank == 1:
+                    store(ot, bt, oh, 1, 2)
+            if last:
+                store(ot, bt, oh, 0, 1)
+            else:
+                store(ot, bt, oh, 0, 2)
+
+        load_x(0)
+        load_w("i", 0)
+        load_w("r", 0)
+        load_x(1)
+        load_w("i", 1)
+        load_w("r", 1)
+        load_x(2)
+        load_x(3)
+
+        tau(0)
+        tau(1)
+        regroup_w("g", "i", 0, 0)
+        regroup_w("v", "r", 0, 0)
+        regroup_w("s", "i", 0, 1)
+        regroup_w("g", "r", 0, 1)
+        quant_w_half(0, 0)
+        quant_w_half(0, 1)
+        for h in range(2):
+            regroup_w("g", "i", 1, h)
+            regroup_w("g", "r", 1, h)
+        tau(2)
+        mu(0, 0, False)
+        tau(3)
+        tau(4)
+        mu(1, 0, False)
+        load_x(4)
+        quant_w_half(1, 0)
+        quant_w_half(1, 1)
+        sort_x(6, 1)
+        tau(5)
+        mu(0, 1, False)
+        sort_x(7, 1)
+        tau(6)
+        mu(1, 1, False)
+        load_x(5)
+        u = 7
+        for bt in range(2, NBT):
+            for oh in range(2):
+                if u < 2 * NBT:
+                    if u + 1 < 2 * NBT:
+                        sort_x(u + 1, 1)
+                    tau(u)
+                    u += 1
+                mu(bt, oh, bt == NBT - 1 and oh == 1)
+            if bt + 4 < NBT:
+                load_x(bt + 4)

@@ -8,12 +8,11 @@ BF16 = mybir.dt.bfloat16
 U32 = mybir.dt.uint32
 U8 = mybir.dt.uint8
 FP8X4 = mybir.dt.float8_e4m3fn_x4
-MULT = mybir.AluOpType.mult
-ADD = mybir.AluOpType.add
 
 P = 128
 B, I, O, NM = 1024, 512, 256, 8
 NBT = B // P
+NU = 2 * NBT
 FLOPS = 2 * 4 * NM * B * I * O
 
 
@@ -33,9 +32,9 @@ def tile_mymodel_t_kernel(tc, x_real, x_imag, w_real, w_imag, out):
         const = ctx.enter_context(tc.tile_pool(name="const", bufs=1))
         big = ctx.enter_context(tc.tile_pool(name="big", bufs=10))
         wpool = ctx.enter_context(tc.tile_pool(name="wpool", bufs=1))
-        spool = ctx.enter_context(tc.tile_pool(name="spool", bufs=4))
+        wgpool = ctx.enter_context(tc.tile_pool(name="wgpool", bufs=6))
         gpool = ctx.enter_context(tc.tile_pool(name="gpool", bufs=2))
-        cpool = ctx.enter_context(tc.tile_pool(name="cpool", bufs=8))
+        cpool = ctx.enter_context(tc.tile_pool(name="cpool", bufs=10))
         opool = ctx.enter_context(tc.tile_pool(name="opool", bufs=3))
         ps_t = ctx.enter_context(tc.psum_pool(name="ps_t", bufs=4))
         ps_o = ctx.enter_context(tc.psum_pool(name="ps_o", bufs=4))
@@ -56,11 +55,7 @@ def tile_mymodel_t_kernel(tc, x_real, x_imag, w_real, w_imag, out):
 
         def load_w(v, oh):
             wt = big.tile([P, 4, P * NM], BF16, name="wt", tag="big")
-            for u in range(2):
-                nc.sync.dma_start(
-                    out=wt[:, 2 * u : 2 * u + 2, :],
-                    in_=w_dram[v][:, 2 * u : 2 * u + 2, oh * P * NM : (oh + 1) * P * NM],
-                )
+            nc.sync.dma_start(out=wt[:], in_=w_dram[v][:, :, oh * P * NM : (oh + 1) * P * NM])
             w_raw[(v, oh)] = wt
 
         w_codes = {}
@@ -73,16 +68,19 @@ def tile_mymodel_t_kernel(tc, x_real, x_imag, w_real, w_imag, out):
         w_grouped = {}
 
         def regroup_w(eng, v, oh, h):
-            g = wpool.tile([P, 2048], BF16, name="g_%s%d" % (v, h), align_bytes=64)
+            g = wgpool.tile([P, 2048], BF16, name="g", align_bytes=64)
             w_grouped[(v, oh, h)] = g
             o_ap = g[:].rearrange("p (m o t) -> p o t m", m=4, t=4)
             i_ap = w_raw[(v, oh)][:].rearrange("p t (o m) -> p o t m", m=NM)[:, :, :, 4 * h : 4 * h + 4]
             if eng == "v":
                 nc.vector.tensor_copy(out=o_ap, in_=i_ap)
-            elif eng == "s":
-                nc.scalar.copy(out=o_ap, in_=i_ap)
             else:
-                nc.gpsimd.tensor_scalar(out=o_ap, in0=i_ap, scalar1=1.0, scalar2=0.0, op0=MULT, op1=ADD)
+                nc.scalar.copy(out=o_ap, in_=i_ap)
+
+        def negate_w(oh, h):
+            gn = wgpool.tile([P, 2048], BF16, name="g", align_bytes=64)
+            w_grouped[("n", oh, h)] = gn
+            nc.vector.tensor_scalar_mul(out=gn[:], in0=w_grouped[("i", oh, h)][:], scalar1=-1.0)
 
         def quant_w(v, oh, h):
             cols = slice(h * 512, (h + 1) * 512)
@@ -92,66 +90,43 @@ def tile_mymodel_t_kernel(tc, x_real, x_imag, w_real, w_imag, out):
                 in_=w_grouped[(v, oh, h)][:],
             )
 
-        def quant_w_half(oh, h):
-            quant_w("i", oh, h)
-            gn = wpool.tile([P, 2048], BF16, name="g_n%d" % h, align_bytes=64)
-            w_grouped[("n", oh, h)] = gn
-            nc.vector.tensor_scalar_mul(out=gn[:], in0=w_grouped[("i", oh, h)][:], scalar1=-1.0)
-            quant_w("r", oh, h)
-            quant_w("n", oh, h)
-
-        x_sorted = {}
-
-        def sort_x(u, s):
-            bt, h = u // 2, u % 2
-            xs = spool.tile([P, 4 * I], BF16, name="xs")
-            nc.gpsimd.tensor_scalar(
-                out=xs[:].rearrange("p (m i) -> p i m", m=4),
-                in0=x_tiles[(bt, s)][:].rearrange("p (i m) -> p i m", m=NM)[:, :, 4 * h : 4 * h + 4],
-                scalar1=1.0,
-                scalar2=0.0,
-                op0=MULT,
-                op1=ADD,
-            )
-            x_sorted[(u, s)] = xs
-
         x_codes = {}
+        x_banks = {}
+        x_grouped = {}
 
-        def tau(u):
+        def turn(u, s):
             bt, h = u // 2, u % 2
-            grouped = gpool.tile([P, 4096], BF16, name="grouped", align_bytes=64)
-            banks = []
-            for s in range(2):
-                if (u, s) in x_sorted:
-                    xw = x_sorted[(u, s)][:].bitcast(F32).rearrange("p (m j u) -> p m u j", m=4, u=2)
-                else:
-                    xw = x_tiles[(bt, s)][:].bitcast(F32).rearrange("p (j u e q) -> p u e q j", u=2, e=2, q=4)
-                for mpl in range(2):
-                    tb = ps_t.tile([P, 512], F32, name="tb")
-                    for t in range(4):
-                        if (u, s) in x_sorted:
-                            src = xw[:, 2 * mpl + t // 2, t % 2, :]
-                        else:
-                            src = xw[:, t // 2, t % 2, 2 * h + mpl, :]
-                        nc.tensor.transpose(tb[:, t * P : (t + 1) * P], src, ident[:])
-                    banks.append(tb)
-            for k in range(4):
-                part = grouped[:, k * 1024 : (k + 1) * 1024]
-                if (u, k // 2) in x_sorted:
-                    o_ap = part.bitcast(F32).rearrange("p (m b u) -> p m b u", m=2, u=2)
-                    i_ap = banks[k][:].rearrange("p (m u b) -> p m b u", m=2, u=2)
-                else:
-                    o_ap = part.rearrange("p (m b t) -> p m b t", m=2, t=4)
-                    i_ap = banks[k][:].bitcast(BF16).rearrange("p (t b m) -> p m b t", t=4, m=2)
-                on_vector = (k == 3) if u < 6 else (k % 2 == 1)
-                if on_vector:
-                    nc.vector.tensor_copy(out=o_ap, in_=i_ap)
-                else:
-                    nc.scalar.copy(out=o_ap, in_=i_ap)
+            xw = x_tiles[(bt, s)][:].bitcast(F32).rearrange("p (j t q) -> p t q j", t=4, q=4)
+            for mpl in range(2):
+                tb = ps_t.tile([P, 512], F32, name="tb")
+                for t in range(4):
+                    nc.tensor.transpose(tb[:, t * P : (t + 1) * P], xw[:, t, 2 * h + mpl, :], ident[:])
+                x_banks[(u, s, mpl)] = tb
+
+        def drain(u, s, mpl, eng):
+            if u not in x_grouped:
+                x_grouped[u] = gpool.tile([P, 4096], BF16, name="grouped", align_bytes=64)
+            k = 2 * s + mpl
+            part = x_grouped[u][:, k * 1024 : (k + 1) * 1024]
+            bank = x_banks[(u, s, mpl)]
+            o_ap = part.rearrange("p (m b t) -> p m b t", m=2, t=4)
+            i_ap = bank[:].bitcast(BF16).rearrange("p (t b m) -> p m b t", t=4, m=2)
+            if eng == "v":
+                nc.vector.tensor_copy(out=o_ap, in_=i_ap)
+            else:
+                nc.scalar.copy(out=o_ap, in_=i_ap)
+
+        def quant_x(u):
             xc = cpool.tile([P, 1024], U32, name="xc", align_bytes=64)
             xsc = cpool.tile([P, 1024], U8, name="xsc", align_bytes=64)
-            nc.vector.quantize_mx(out=xc[:].bitcast(FP8X4), scales=xsc[:], in_=grouped[:])
+            nc.vector.quantize_mx(out=xc[:].bitcast(FP8X4), scales=xsc[:], in_=x_grouped[u][:])
             x_codes[u] = (xc, xsc)
+
+        def tau(u, engs):
+            for s in range(2):
+                turn(u, s)
+            for k in range(4):
+                drain(u, k // 2, k % 2, engs[k])
 
         def store(ot, bt, oh, c0, c1):
             nc.sync.dma_start(
@@ -159,7 +134,7 @@ def tile_mymodel_t_kernel(tc, x_real, x_imag, w_real, w_imag, out):
                 in_=ot[:, c0:c1].rearrange("p c o m -> p c (o m)"),
             )
 
-        def mu(bt, oh, last):
+        def mu(bt, oh, engs, last=False):
             ot = opool.tile([P, 2, P, NM], F32, name="ot")
             order = ((1, 0), (1, 1), (0, 0), (0, 1)) if last else ((1, 0), (0, 0), (1, 1), (0, 1))
             for n_bank, (c, h) in enumerate(order):
@@ -181,7 +156,7 @@ def tile_mymodel_t_kernel(tc, x_real, x_imag, w_real, w_imag, out):
                         )
                 o_ap = ot[:, c, :, 4 * h : 4 * h + 4]
                 i_ap = ob[:].rearrange("p (m o) -> p o m", m=4)
-                if c == 0 and oh == 0 and bt >= 2:
+                if engs[n_bank] == "v":
                     nc.vector.tensor_copy(out=o_ap, in_=i_ap)
                 else:
                     nc.scalar.copy(out=o_ap, in_=i_ap)
@@ -192,8 +167,8 @@ def tile_mymodel_t_kernel(tc, x_real, x_imag, w_real, w_imag, out):
             else:
                 store(ot, bt, oh, 0, 2)
 
-        load_x(0)
         load_w("i", 0)
+        load_x(0)
         load_w("r", 0)
         load_x(1)
         load_w("i", 1)
@@ -201,40 +176,56 @@ def tile_mymodel_t_kernel(tc, x_real, x_imag, w_real, w_imag, out):
         load_x(2)
         load_x(3)
 
-        tau(0)
-        tau(1)
-        regroup_w("g", "i", 0, 0)
-        regroup_w("v", "r", 0, 0)
+        regroup_w("v", "i", 0, 0)
         regroup_w("s", "i", 0, 1)
-        regroup_w("g", "r", 0, 1)
-        quant_w_half(0, 0)
-        quant_w_half(0, 1)
-        for h in range(2):
-            regroup_w("g", "i", 1, h)
-            regroup_w("g", "r", 1, h)
-        tau(2)
-        mu(0, 0, False)
-        tau(3)
-        tau(4)
-        mu(1, 0, False)
-        load_x(4)
-        quant_w_half(1, 0)
-        quant_w_half(1, 1)
-        sort_x(6, 1)
-        tau(5)
-        mu(0, 1, False)
-        sort_x(7, 1)
-        tau(6)
-        mu(1, 1, False)
-        load_x(5)
-        u = 7
-        for bt in range(2, NBT):
-            for oh in range(2):
-                if u < 2 * NBT:
-                    if u + 1 < 2 * NBT:
-                        sort_x(u + 1, 1)
-                    tau(u)
-                    u += 1
-                mu(bt, oh, bt == NBT - 1 and oh == 1)
-            if bt + 4 < NBT:
-                load_x(bt + 4)
+        turn(0, 0)
+        turn(1, 0)
+        quant_w("i", 0, 0)
+        negate_w(0, 0)
+        negate_w(0, 1)
+        quant_w("i", 0, 1)
+        quant_w("n", 0, 0)
+        quant_w("n", 0, 1)
+        drain(0, 0, 0, "s")
+        drain(0, 0, 1, "s")
+        turn(0, 1)
+        drain(1, 0, 0, "v")
+        drain(1, 0, 1, "s")
+        turn(1, 1)
+        drain(0, 1, 0, "v")
+        drain(0, 1, 1, "s")
+        regroup_w("v", "r", 0, 0)
+        quant_x(0)
+        drain(1, 1, 0, "v")
+        drain(1, 1, 1, "s")
+        quant_w("r", 0, 0)
+        regroup_w("v", "r", 0, 1)
+        quant_x(1)
+        quant_w("r", 0, 1)
+
+        mus = [(bt, oh) for oh in range(2) for bt in range(3)]
+        mus += [(bt, oh) for bt in range(3, NBT) for oh in range(2)]
+        done = 2
+        loaded = 4
+        for j, (bt, oh) in enumerate(mus):
+            need = 2 * max(b for b, o in mus[: j + 2]) + 2
+            need = min(NU, max(need, done + 1))
+            while done < need:
+                if loaded < NBT and loaded <= done // 2 + 3:
+                    load_x(loaded)
+                    loaded += 1
+                tau(done, "sssv")
+                if done - 1 not in x_codes:
+                    quant_x(done - 1)
+                done += 1
+            if j in (1, 2):
+                h = j - 1
+                regroup_w("v", "i", 1, h)
+                regroup_w("v", "r", 1, h)
+                negate_w(1, h)
+                quant_w("i", 1, h)
+                quant_w("r", 1, h)
+                quant_w("n", 1, h)
+            mu(bt, oh, "ssss" if j < 3 else "vsss", j == len(mus) - 1)
+            if done - 1 not in x_codes:
+                quant_x(done - 1)

@@ -13,6 +13,7 @@ P = 128
 B, I, O, NM = 1024, 512, 256, 8
 NBT = B // P
 NU = 2 * NBT
+FIRST_SORTED = 6
 FLOPS = 2 * 4 * NM * B * I * O
 
 
@@ -30,11 +31,12 @@ def tile_mymodel_t_kernel(tc, x_real, x_imag, w_real, w_imag, out):
 
     with ExitStack() as ctx:
         const = ctx.enter_context(tc.tile_pool(name="const", bufs=1))
-        big = ctx.enter_context(tc.tile_pool(name="big", bufs=10))
+        big = ctx.enter_context(tc.tile_pool(name="big", bufs=9))
         wpool = ctx.enter_context(tc.tile_pool(name="wpool", bufs=1))
-        wgpool = ctx.enter_context(tc.tile_pool(name="wgpool", bufs=6))
+        wgpool = ctx.enter_context(tc.tile_pool(name="wgpool", bufs=3))
         gpool = ctx.enter_context(tc.tile_pool(name="gpool", bufs=2))
-        cpool = ctx.enter_context(tc.tile_pool(name="cpool", bufs=10))
+        cpool = ctx.enter_context(tc.tile_pool(name="cpool", bufs=9))
+        spool = ctx.enter_context(tc.tile_pool(name="spool", bufs=6))
         opool = ctx.enter_context(tc.tile_pool(name="opool", bufs=3))
         ps_t = ctx.enter_context(tc.psum_pool(name="ps_t", bufs=4))
         ps_o = ctx.enter_context(tc.psum_pool(name="ps_o", bufs=4))
@@ -68,9 +70,10 @@ def tile_mymodel_t_kernel(tc, x_real, x_imag, w_real, w_imag, out):
         w_grouped = {}
 
         def regroup_w(eng, v, oh, h):
-            g = wgpool.tile([P, 2048], BF16, name="g", align_bytes=64)
-            w_grouped[(v, oh, h)] = g
-            o_ap = g[:].rearrange("p (m o t) -> p o t m", m=4, t=4)
+            if (v, oh) not in w_grouped:
+                w_grouped[(v, oh)] = wgpool.tile([P, 4096], BF16, name="g", align_bytes=64)
+            g = w_grouped[(v, oh)][:, h * 2048 : (h + 1) * 2048]
+            o_ap = g.rearrange("p (m o t) -> p o t m", m=4, t=4)
             i_ap = w_raw[(v, oh)][:].rearrange("p t (o m) -> p o t m", m=NM)[:, :, :, 4 * h : 4 * h + 4]
             if eng == "v":
                 nc.vector.tensor_copy(out=o_ap, in_=i_ap)
@@ -78,17 +81,29 @@ def tile_mymodel_t_kernel(tc, x_real, x_imag, w_real, w_imag, out):
                 nc.scalar.copy(out=o_ap, in_=i_ap)
 
         def negate_w(oh, h):
-            gn = wgpool.tile([P, 2048], BF16, name="g", align_bytes=64)
-            w_grouped[("n", oh, h)] = gn
-            nc.vector.tensor_scalar_mul(out=gn[:], in0=w_grouped[("i", oh, h)][:], scalar1=-1.0)
+            if ("n", oh) not in w_grouped:
+                w_grouped[("n", oh)] = wgpool.tile([P, 4096], BF16, name="g", align_bytes=64)
+            cols = slice(h * 2048, (h + 1) * 2048)
+            nc.vector.tensor_scalar_mul(out=w_grouped[("n", oh)][:, cols], in0=w_grouped[("i", oh)][:, cols], scalar1=-1.0)
 
         def quant_w(v, oh, h):
             cols = slice(h * 512, (h + 1) * 512)
             nc.vector.quantize_mx(
                 out=w_codes[(v, oh)][:, cols].bitcast(FP8X4),
                 scales=w_scales[(v, oh)][:, cols],
-                in_=w_grouped[(v, oh, h)][:],
+                in_=w_grouped[(v, oh)][:, h * 2048 : (h + 1) * 2048],
             )
+
+        x_sorted = {}
+
+        def sort_x(u, s):
+            bt, h = u // 2, u % 2
+            xs = spool.tile([P, 4 * I], BF16, name="xs")
+            for uu in range(2):
+                o_ap = xs[:].rearrange("p (m u j e) -> p u j e m", m=4, u=2, e=2)[:, uu]
+                i_ap = x_tiles[(bt, s)][:].rearrange("p (j u e m) -> p u j e m", u=2, e=2, m=NM)[:, uu, :, :, 4 * h : 4 * h + 4]
+                nc.vector.tensor_copy(out=o_ap, in_=i_ap)
+            x_sorted[(u, s)] = xs
 
         x_codes = {}
         x_banks = {}
@@ -97,10 +112,16 @@ def tile_mymodel_t_kernel(tc, x_real, x_imag, w_real, w_imag, out):
         def turn(u, s):
             bt, h = u // 2, u % 2
             xw = x_tiles[(bt, s)][:].bitcast(F32).rearrange("p (j t q) -> p t q j", t=4, q=4)
+            if (u, s) in x_sorted:
+                xw = x_sorted[(u, s)][:].bitcast(F32).rearrange("p (m u j) -> p m u j", m=4, u=2)
             for mpl in range(2):
                 tb = ps_t.tile([P, 512], F32, name="tb")
                 for t in range(4):
-                    nc.tensor.transpose(tb[:, t * P : (t + 1) * P], xw[:, t, 2 * h + mpl, :], ident[:])
+                    if (u, s) in x_sorted:
+                        src = xw[:, 2 * mpl + t // 2, t % 2, :]
+                    else:
+                        src = xw[:, t, 2 * h + mpl, :]
+                    nc.tensor.transpose(tb[:, t * P : (t + 1) * P], src, ident[:])
                 x_banks[(u, s, mpl)] = tb
 
         def drain(u, s, mpl, eng):
@@ -111,6 +132,9 @@ def tile_mymodel_t_kernel(tc, x_real, x_imag, w_real, w_imag, out):
             bank = x_banks[(u, s, mpl)]
             o_ap = part.rearrange("p (m b t) -> p m b t", m=2, t=4)
             i_ap = bank[:].bitcast(BF16).rearrange("p (t b m) -> p m b t", t=4, m=2)
+            if (u, s) in x_sorted:
+                o_ap = part.bitcast(F32).rearrange("p (m b u) -> p m b u", m=2, u=2)
+                i_ap = bank[:].rearrange("p (m u b) -> p m b u", m=2, u=2)
             if eng == "v":
                 nc.vector.tensor_copy(out=o_ap, in_=i_ap)
             else:
@@ -203,29 +227,33 @@ def tile_mymodel_t_kernel(tc, x_real, x_imag, w_real, w_imag, out):
         quant_x(1)
         quant_w("r", 0, 1)
 
-        mus = [(bt, oh) for oh in range(2) for bt in range(3)]
-        mus += [(bt, oh) for bt in range(3, NBT) for oh in range(2)]
+        mus = [(bt, oh) for oh in range(2) for bt in range(2)]
+        mus += [(bt, oh) for bt in range(2, NBT) for oh in range(2)]
         done = 2
+        sd = FIRST_SORTED
         loaded = 4
         for j, (bt, oh) in enumerate(mus):
-            need = 2 * max(b for b, o in mus[: j + 2]) + 2
+            need = 2 * max(b for b, o in mus[: j + 3]) + 2
             need = min(NU, max(need, done + 1))
             while done < need:
                 if loaded < NBT and loaded <= done // 2 + 3:
                     load_x(loaded)
                     loaded += 1
-                tau(done, "sssv")
+                while sd < NU and sd <= done + 1:
+                    for s in range(2):
+                        sort_x(sd, s)
+                    sd += 1
+                tau(done, "sssv" if done > FIRST_SORTED and done % 2 == 1 else "ssss")
                 if done - 1 not in x_codes:
                     quant_x(done - 1)
                 done += 1
-            if j in (1, 2):
-                h = j - 1
-                regroup_w("v", "i", 1, h)
-                regroup_w("v", "r", 1, h)
-                negate_w(1, h)
-                quant_w("i", 1, h)
-                quant_w("r", 1, h)
-                quant_w("n", 1, h)
-            mu(bt, oh, "ssss" if j < 3 else "vsss", j == len(mus) - 1)
+            if j < 2:
+                regroup_w("v", "i", 1, j)
+                negate_w(1, j)
+                quant_w("i", 1, j)
+                quant_w("n", 1, j)
+                regroup_w("v", "r", 1, j)
+                quant_w("r", 1, j)
+            mu(bt, oh, "ssss", j == len(mus) - 1)
             if done - 1 not in x_codes:
                 quant_x(done - 1)

@@ -31,11 +31,11 @@ def tile_mymodel_t_kernel(tc, x_real, x_imag, w_real, w_imag, out):
 
     with ExitStack() as ctx:
         const = ctx.enter_context(tc.tile_pool(name="const", bufs=1))
-        big = ctx.enter_context(tc.tile_pool(name="big", bufs=9))
+        big = ctx.enter_context(tc.tile_pool(name="big", bufs=8))
         wpool = ctx.enter_context(tc.tile_pool(name="wpool", bufs=1))
         wgpool = ctx.enter_context(tc.tile_pool(name="wgpool", bufs=3))
         gpool = ctx.enter_context(tc.tile_pool(name="gpool", bufs=2))
-        cpool = ctx.enter_context(tc.tile_pool(name="cpool", bufs=9))
+        cpool = ctx.enter_context(tc.tile_pool(name="cpool", bufs=8))
         spool = ctx.enter_context(tc.tile_pool(name="spool", bufs=6))
         opool = ctx.enter_context(tc.tile_pool(name="opool", bufs=3))
         ps_t = ctx.enter_context(tc.psum_pool(name="ps_t", bufs=4))
@@ -55,9 +55,14 @@ def tile_mymodel_t_kernel(tc, x_real, x_imag, w_real, w_imag, out):
 
         w_raw = {}
 
-        def load_w(v, oh):
+        def load_w(v, oh, parts=1):
             wt = big.tile([P, 4, P * NM], BF16, name="wt", tag="big")
-            nc.sync.dma_start(out=wt[:], in_=w_dram[v][:, :, oh * P * NM : (oh + 1) * P * NM])
+            width = P * NM // parts
+            for k in range(parts):
+                nc.sync.dma_start(
+                    out=wt[:, :, k * width : (k + 1) * width],
+                    in_=w_dram[v][:, :, oh * P * NM + k * width : oh * P * NM + (k + 1) * width],
+                )
             w_raw[(v, oh)] = wt
 
         w_codes = {}
@@ -69,12 +74,12 @@ def tile_mymodel_t_kernel(tc, x_real, x_imag, w_real, w_imag, out):
 
         w_grouped = {}
 
-        def regroup_w(eng, v, oh, h):
+        def regroup_w(eng, v, oh, h, o0=0, o1=P):
             if (v, oh) not in w_grouped:
                 w_grouped[(v, oh)] = wgpool.tile([P, 4096], BF16, name="g", align_bytes=64)
             g = w_grouped[(v, oh)][:, h * 2048 : (h + 1) * 2048]
-            o_ap = g.rearrange("p (m o t) -> p o t m", m=4, t=4)
-            i_ap = w_raw[(v, oh)][:].rearrange("p t (o m) -> p o t m", m=NM)[:, :, :, 4 * h : 4 * h + 4]
+            o_ap = g.rearrange("p (m o t) -> p o t m", m=4, t=4)[:, o0:o1]
+            i_ap = w_raw[(v, oh)][:].rearrange("p t (o m) -> p o t m", m=NM)[:, o0:o1, :, 4 * h : 4 * h + 4]
             if eng == "v":
                 nc.vector.tensor_copy(out=o_ap, in_=i_ap)
             else:
@@ -191,7 +196,7 @@ def tile_mymodel_t_kernel(tc, x_real, x_imag, w_real, w_imag, out):
             else:
                 store(ot, bt, oh, 0, 2)
 
-        load_w("i", 0)
+        load_w("i", 0, 2)
         load_x(0)
         load_w("r", 0)
         load_x(1)
@@ -200,8 +205,9 @@ def tile_mymodel_t_kernel(tc, x_real, x_imag, w_real, w_imag, out):
         load_x(2)
         load_x(3)
 
-        regroup_w("v", "i", 0, 0)
-        regroup_w("s", "i", 0, 1)
+        for k in range(2):
+            regroup_w("v", "i", 0, 0, 64 * k, 64 * k + 64)
+            regroup_w("s", "i", 0, 1, 64 * k, 64 * k + 64)
         turn(0, 0)
         turn(1, 0)
         quant_w("i", 0, 0)
@@ -233,8 +239,8 @@ def tile_mymodel_t_kernel(tc, x_real, x_imag, w_real, w_imag, out):
         sd = FIRST_SORTED
         loaded = 4
         for j, (bt, oh) in enumerate(mus):
-            need = 2 * max(b for b, o in mus[: j + 3]) + 2
-            need = min(NU, max(need, done + 1))
+            need = 2 * max(b for b, o in mus[: j + 2]) + 2
+            need = min(NU, max(need, done + (j != 4)))
             while done < need:
                 if loaded < NBT and loaded <= done // 2 + 3:
                     load_x(loaded)
@@ -243,7 +249,7 @@ def tile_mymodel_t_kernel(tc, x_real, x_imag, w_real, w_imag, out):
                     for s in range(2):
                         sort_x(sd, s)
                     sd += 1
-                tau(done, "sssv" if done > FIRST_SORTED and done % 2 == 1 else "ssss")
+                tau(done, "sssv" if FIRST_SORTED < done < 12 and done % 2 == 1 else "ssss")
                 if done - 1 not in x_codes:
                     quant_x(done - 1)
                 done += 1
@@ -254,6 +260,6 @@ def tile_mymodel_t_kernel(tc, x_real, x_imag, w_real, w_imag, out):
                 quant_w("n", 1, j)
                 regroup_w("v", "r", 1, j)
                 quant_w("r", 1, j)
-            mu(bt, oh, "ssss", j == len(mus) - 1)
+            mu(bt, oh, "ssss" if j < len(mus) - 4 else "vsvs", j == len(mus) - 1)
             if done - 1 not in x_codes:
                 quant_x(done - 1)

@@ -163,11 +163,14 @@ def tile_mymodel_t_kernel(tc, x_real, x_imag, w_real, w_imag, out):
                 in_=ot[:, c0:c1].rearrange("p c o m -> p c (o m)"),
             )
 
-        def mu(bt, oh, engs, last=False):
-            ot = opool.tile([P, 2, P, NM], F32, name="ot")
-            order = ((1, 0), (1, 1), (0, 0), (0, 1)) if last else ((1, 0), (0, 0), (1, 1), (0, 1))
-            for n_bank, (c, h) in enumerate(order):
-                xc, xsc = x_codes[2 * bt + h]
+        out_tiles = {}
+
+        def mu(bt, oh, h, engs, last):
+            if h == 0:
+                out_tiles[(bt, oh)] = opool.tile([P, 2, P, NM], F32, name="ot")
+            ot = out_tiles[(bt, oh)]
+            xc, xsc = x_codes[2 * bt + h]
+            for c in (1, 0):
                 ob = ps_o.tile([P, 512], F32, name="ob")
                 for ml in range(4):
                     pairs = ((0, "r"), (1, "n")) if c == 0 else ((0, "i"), (1, "r"))
@@ -185,15 +188,13 @@ def tile_mymodel_t_kernel(tc, x_real, x_imag, w_real, w_imag, out):
                         )
                 o_ap = ot[:, c, :, 4 * h : 4 * h + 4]
                 i_ap = ob[:].rearrange("p (m o) -> p o m", m=4)
-                if engs[n_bank] == "v":
+                if engs[1 - c] == "v":
                     nc.vector.tensor_copy(out=o_ap, in_=i_ap)
                 else:
                     nc.scalar.copy(out=o_ap, in_=i_ap)
-                if last and n_bank == 1:
-                    store(ot, bt, oh, 1, 2)
-            if last:
-                store(ot, bt, oh, 0, 1)
-            else:
+                if last and h == 1:
+                    store(ot, bt, oh, c, c + 1)
+            if h == 1 and not last:
                 store(ot, bt, oh, 0, 2)
 
         load_w("i", 0, 2)
@@ -235,31 +236,33 @@ def tile_mymodel_t_kernel(tc, x_real, x_imag, w_real, w_imag, out):
 
         mus = [(bt, oh) for oh in range(2) for bt in range(2)]
         mus += [(bt, oh) for bt in range(2, NBT) for oh in range(2)]
-        done = 2
-        sd = FIRST_SORTED
+        steps = [(bt, oh, h) for bt, oh in mus for h in range(2)]
+        second_half = ((("i", 0),), (("n", 0), ("r", 0)), (("i", 1),), (("n", 1), ("r", 1)))
+        done = 4
+        sorted_to = 2 * FIRST_SORTED
         loaded = 4
-        for j, (bt, oh) in enumerate(mus):
-            need = 2 * max(b for b, o in mus[: j + 2]) + 2
-            need = min(NU, max(need, done + (j != 4)))
+        for k, (bt, oh, h) in enumerate(steps):
+            need = max(2 * (2 * b + hh) + 2 for b, o, hh in steps[: k + 3])
+            need = min(2 * NU, max(need, done + 1))
+            while loaded < NBT and loaded <= done // 4 + 3:
+                load_x(loaded)
+                loaded += 1
             while done < need:
-                if loaded < NBT and loaded <= done // 2 + 3:
-                    load_x(loaded)
-                    loaded += 1
-                while sd < NU and sd <= done + 1:
-                    for s in range(2):
-                        sort_x(sd, s)
-                    sd += 1
-                tau(done, "sssv" if FIRST_SORTED < done < 12 and done % 2 == 1 else "ssss")
-                if done - 1 not in x_codes:
-                    quant_x(done - 1)
+                while sorted_to < 2 * NU and sorted_to <= done + 2:
+                    sort_x(sorted_to // 2, sorted_to % 2)
+                    sorted_to += 1
+                u, s = done // 2, done % 2
+                turn(u, s)
+                drain(u, s, 0, "s")
+                drain(u, s, 1, "s")
                 done += 1
-            if j < 2:
-                regroup_w("v", "i", 1, j)
-                negate_w(1, j)
-                quant_w("i", 1, j)
-                quant_w("n", 1, j)
-                regroup_w("v", "r", 1, j)
-                quant_w("r", 1, j)
-            mu(bt, oh, "ssss" if j < len(mus) - 4 else "vsvs", j == len(mus) - 1)
-            if done - 1 not in x_codes:
-                quant_x(done - 1)
+            if k < 4:
+                for v, hh in second_half[k]:
+                    if v == "n":
+                        negate_w(1, hh)
+                    else:
+                        regroup_w("v", v, 1, hh)
+                    quant_w(v, 1, hh)
+            if done % 2 == 0 and done // 2 - 1 not in x_codes:
+                quant_x(done // 2 - 1)
+            mu(bt, oh, h, "vs" if k >= len(steps) - 4 else "ss", k == len(steps) - 1)

@@ -104,10 +104,9 @@ def tile_mymodel_t_kernel(tc, x_real, x_imag, w_real, w_imag, out):
         def sort_x(u, s):
             bt, h = u // 2, u % 2
             xs = spool.tile([P, 4 * I], BF16, name="xs")
-            for uu in range(2):
-                o_ap = xs[:].rearrange("p (m u j e) -> p u j e m", m=4, u=2, e=2)[:, uu]
-                i_ap = x_tiles[(bt, s)][:].rearrange("p (j u e m) -> p u j e m", u=2, e=2, m=NM)[:, uu, :, :, 4 * h : 4 * h + 4]
-                nc.vector.tensor_copy(out=o_ap, in_=i_ap)
+            o_ap = xs[:].rearrange("p (m u j e) -> p u j e m", m=4, u=2, e=2)
+            i_ap = x_tiles[(bt, s)][:].rearrange("p (j u e m) -> p u j e m", u=2, e=2, m=NM)[:, :, :, :, 4 * h : 4 * h + 4]
+            nc.vector.tensor_copy(out=o_ap, in_=i_ap)
             x_sorted[(u, s)] = xs
 
         x_codes = {}
@@ -151,12 +150,6 @@ def tile_mymodel_t_kernel(tc, x_real, x_imag, w_real, w_imag, out):
             nc.vector.quantize_mx(out=xc[:].bitcast(FP8X4), scales=xsc[:], in_=x_grouped[u][:])
             x_codes[u] = (xc, xsc)
 
-        def tau(u, engs):
-            for s in range(2):
-                turn(u, s)
-            for k in range(4):
-                drain(u, k // 2, k % 2, engs[k])
-
         def store(ot, bt, oh, c0, c1):
             nc.sync.dma_start(
                 out=out_dram[bt * P : (bt + 1) * P, c0:c1, oh * P * NM : (oh + 1) * P * NM],
@@ -197,7 +190,7 @@ def tile_mymodel_t_kernel(tc, x_real, x_imag, w_real, w_imag, out):
             if h == 1 and not last:
                 store(ot, bt, oh, 0, 2)
 
-        load_w("i", 0, 2)
+        load_w("i", 0, 4)
         load_x(0)
         load_w("r", 0)
         load_x(1)
@@ -206,9 +199,9 @@ def tile_mymodel_t_kernel(tc, x_real, x_imag, w_real, w_imag, out):
         load_x(2)
         load_x(3)
 
-        for k in range(2):
-            regroup_w("v", "i", 0, 0, 64 * k, 64 * k + 64)
-            regroup_w("s", "i", 0, 1, 64 * k, 64 * k + 64)
+        for k in range(4):
+            regroup_w("v", "i", 0, 0, P // 4 * k, P // 4 * (k + 1))
+            regroup_w("s", "i", 0, 1, P // 4 * k, P // 4 * (k + 1))
         turn(0, 0)
         turn(1, 0)
         quant_w("i", 0, 0)
@@ -227,7 +220,7 @@ def tile_mymodel_t_kernel(tc, x_real, x_imag, w_real, w_imag, out):
         drain(0, 1, 1, "s")
         regroup_w("v", "r", 0, 0)
         quant_x(0)
-        drain(1, 1, 0, "v")
+        drain(1, 1, 0, "s")
         drain(1, 1, 1, "s")
         quant_w("r", 0, 0)
         regroup_w("v", "r", 0, 1)
@@ -237,14 +230,15 @@ def tile_mymodel_t_kernel(tc, x_real, x_imag, w_real, w_imag, out):
         mus = [(bt, oh) for oh in range(2) for bt in range(2)]
         mus += [(bt, oh) for bt in range(2, NBT) for oh in range(2)]
         steps = [(bt, oh, h) for bt, oh in mus for h in range(2)]
-        second_half = ((("i", 0),), (("n", 0), ("r", 0)), (("i", 1),), (("n", 1), ("r", 1)))
         done = 4
         sorted_to = 2 * FIRST_SORTED
         loaded = 4
+        w2 = [("i", 0), ("n", 0), ("r", 0), ("i", 1), ("n", 1), ("r", 1)]
+        w2_count = (0, 1, 2, 1, 2)
         for k, (bt, oh, h) in enumerate(steps):
-            need = max(2 * (2 * b + hh) + 2 for b, o, hh in steps[: k + 3])
-            need = min(2 * NU, max(need, done + 1))
-            while loaded < NBT and loaded <= done // 4 + 3:
+            ahead = max(2 * (2 * b + hh) + 2 for b, o, hh in steps[: k + 2])
+            need = min(2 * NU, max(ahead, done + 1))
+            while loaded < NBT and loaded <= done // 4 + 2:
                 load_x(loaded)
                 loaded += 1
             while done < need:
@@ -256,13 +250,16 @@ def tile_mymodel_t_kernel(tc, x_real, x_imag, w_real, w_imag, out):
                 drain(u, s, 0, "s")
                 drain(u, s, 1, "s")
                 done += 1
-            if k < 4:
-                for v, hh in second_half[k]:
-                    if v == "n":
-                        negate_w(1, hh)
-                    else:
-                        regroup_w("v", v, 1, hh)
-                    quant_w(v, 1, hh)
-            if done % 2 == 0 and done // 2 - 1 not in x_codes:
+                if done % 2 == 1 and done // 2 - 1 not in x_codes:
+                    quant_x(done // 2 - 1)
+            for v, hh in w2[sum(w2_count[:k]) : sum(w2_count[: k + 1])]:
+                if v == "n":
+                    negate_w(1, hh)
+                else:
+                    regroup_w("v", v, 1, hh)
+                quant_w(v, 1, hh)
+            if 2 * bt + h not in x_codes:
+                quant_x(2 * bt + h)
+            mu(bt, oh, h, "sv" if h == 1 else "ss", k == len(steps) - 1)
+            if done // 2 - 1 not in x_codes and done % 2 == 0:
                 quant_x(done // 2 - 1)
-            mu(bt, oh, h, "vs" if k >= len(steps) - 4 else "ss", k == len(steps) - 1)

@@ -150,20 +150,17 @@ def tile_mymodel_t_kernel(tc, x_real, x_imag, w_real, w_imag, out):
             nc.vector.quantize_mx(out=xc[:].bitcast(FP8X4), scales=xsc[:], in_=x_grouped[u][:])
             x_codes[u] = (xc, xsc)
 
-        def store(ot, bt, oh, c0, c1):
-            nc.sync.dma_start(
-                out=out_dram[bt * P : (bt + 1) * P, c0:c1, oh * P * NM : (oh + 1) * P * NM],
-                in_=ot[:, c0:c1].rearrange("p c o m -> p c (o m)"),
-            )
-
         out_tiles = {}
 
-        def mu(bt, oh, h, engs, last):
+        def out_piece(bt, c, oh):
+            return out_dram[bt * P : (bt + 1) * P, c, oh * P * NM : (oh + 1) * P * NM]
+
+        def mu(bt, banks, h, engs, last):
             if h == 0:
-                out_tiles[(bt, oh)] = opool.tile([P, 2, P, NM], F32, name="ot")
-            ot = out_tiles[(bt, oh)]
+                out_tiles[(bt, banks)] = opool.tile([P, 2, P, NM], F32, name="ot")
+            ot = out_tiles[(bt, banks)]
             xc, xsc = x_codes[2 * bt + h]
-            for c in (1, 0):
+            for k, (c, oh) in enumerate(banks):
                 ob = ps_o.tile([P, 512], F32, name="ob")
                 for ml in range(4):
                     pairs = ((0, "r"), (1, "n")) if c == 0 else ((0, "i"), (1, "r"))
@@ -179,18 +176,25 @@ def tile_mymodel_t_kernel(tc, x_real, x_imag, w_real, w_imag, out):
                             start=(n == 0),
                             stop=(n == 1),
                         )
-                o_ap = ot[:, c, :, 4 * h : 4 * h + 4]
+                o_ap = ot[:, k, :, 4 * h : 4 * h + 4]
                 i_ap = ob[:].rearrange("p (m o) -> p o m", m=4)
-                if engs[1 - c] == "v":
+                if engs[k] == "v":
                     nc.vector.tensor_copy(out=o_ap, in_=i_ap)
                 else:
                     nc.scalar.copy(out=o_ap, in_=i_ap)
                 if last and h == 1:
-                    store(ot, bt, oh, c, c + 1)
+                    nc.sync.dma_start(out=out_piece(bt, c, oh), in_=ot[:, k].rearrange("p o m -> p (o m)"))
             if h == 1 and not last:
-                store(ot, bt, oh, 0, 2)
+                (c0, h0), (c1, h1) = banks
+                if c0 == c1:
+                    nc.sync.dma_start(out=out_dram[bt * P : (bt + 1) * P, c0, :], in_=ot[:].rearrange("p k o m -> p (k o m)"))
+                else:
+                    nc.sync.dma_start(
+                        out=out_dram[bt * P : (bt + 1) * P, :, h0 * P * NM : (h0 + 1) * P * NM],
+                        in_=ot[:].rearrange("p k o m -> p k (o m)"),
+                    )
 
-        load_w("i", 0, 4)
+        load_w("i", 0)
         load_x(0)
         load_w("r", 0)
         load_x(1)
@@ -199,9 +203,8 @@ def tile_mymodel_t_kernel(tc, x_real, x_imag, w_real, w_imag, out):
         load_x(2)
         load_x(3)
 
-        for k in range(4):
-            regroup_w("v", "i", 0, 0, P // 4 * k, P // 4 * (k + 1))
-            regroup_w("s", "i", 0, 1, P // 4 * k, P // 4 * (k + 1))
+        regroup_w("v", "i", 0, 0)
+        regroup_w("s", "i", 0, 1)
         turn(0, 0)
         turn(1, 0)
         quant_w("i", 0, 0)
@@ -227,15 +230,15 @@ def tile_mymodel_t_kernel(tc, x_real, x_imag, w_real, w_imag, out):
         quant_x(1)
         quant_w("r", 0, 1)
 
-        mus = [(bt, oh) for oh in range(2) for bt in range(2)]
-        mus += [(bt, oh) for bt in range(2, NBT) for oh in range(2)]
-        steps = [(bt, oh, h) for bt, oh in mus for h in range(2)]
+        mus = [(bt, ((0, oh), (1, oh))) for oh in range(2) for bt in range(2)]
+        mus += [(bt, ((c, 0), (c, 1))) for bt in range(2, NBT) for c in range(2)]
+        steps = [(bt, banks, h) for bt, banks in mus for h in range(2)]
         done = 4
         sorted_to = 2 * FIRST_SORTED
         loaded = 4
         w2 = [("i", 0), ("n", 0), ("r", 0), ("i", 1), ("n", 1), ("r", 1)]
         w2_count = (0, 1, 2, 1, 2)
-        for k, (bt, oh, h) in enumerate(steps):
+        for k, (bt, banks, h) in enumerate(steps):
             ahead = max(2 * (2 * b + hh) + 2 for b, o, hh in steps[: k + 2])
             need = min(2 * NU, max(ahead, done + 1))
             while loaded < NBT and loaded <= done // 4 + 2:
@@ -260,6 +263,6 @@ def tile_mymodel_t_kernel(tc, x_real, x_imag, w_real, w_imag, out):
                 quant_w(v, 1, hh)
             if 2 * bt + h not in x_codes:
                 quant_x(2 * bt + h)
-            mu(bt, oh, h, "sv" if h == 1 else "ss", k == len(steps) - 1)
+            mu(bt, banks, h, "sv" if h == 1 else "ss", k == len(steps) - 1)
             if done // 2 - 1 not in x_codes and done % 2 == 0:
                 quant_x(done // 2 - 1)

@@ -234,22 +234,30 @@ def tile_mymodel_t_kernel(tc, x_real, x_imag, w_real, w_imag, out):
         mus += [(bt, ((c, 0), (c, 1))) for bt in range(2, NBT) for c in range(2)]
         steps = [(bt, banks, h) for bt, banks in mus for h in range(2)]
         done = 4
+        turned = 4
         sorted_to = 2 * FIRST_SORTED
         loaded = 4
         w2 = [("i", 0), ("n", 0), ("r", 0), ("i", 1), ("n", 1), ("r", 1)]
         w2_count = (0, 1, 2, 1, 2)
-        for k, (bt, banks, h) in enumerate(steps):
+
+        def goal(k, at):
             ahead = max(2 * (2 * b + hh) + 2 for b, o, hh in steps[: k + 2])
-            need = min(2 * NU, max(ahead, done + 1))
+            return min(2 * NU, max(ahead, at + 1))
+
+        for k, (bt, banks, h) in enumerate(steps):
             while loaded < NBT and loaded <= done // 4 + 2:
                 load_x(loaded)
                 loaded += 1
-            while done < need:
-                while sorted_to < 2 * NU and sorted_to <= done + 2:
+            need = goal(k, done)
+            turn_to = goal(k + 1, need) if bt >= 2 and k % 2 == 0 else need
+            while turned < turn_to:
+                while sorted_to < 2 * NU and sorted_to <= turned + 2:
                     sort_x(sorted_to // 2, sorted_to % 2)
                     sorted_to += 1
+                turn(turned // 2, turned % 2)
+                turned += 1
+            while done < need:
                 u, s = done // 2, done % 2
-                turn(u, s)
                 drain(u, s, 0, "s")
                 drain(u, s, 1, "s")
                 done += 1

@@ -14,6 +14,7 @@ B, I, O, NM = 1024, 512, 256, 8
 NBT = B // P
 NU = 2 * NBT
 FIRST_SORTED = 6
+DIRECT = (3, 5)
 FLOPS = 2 * 4 * NM * B * I * O
 
 
@@ -37,13 +38,15 @@ def tile_mymodel_t_kernel(tc, x_real, x_imag, w_real, w_imag, out):
         gpool = ctx.enter_context(tc.tile_pool(name="gpool", bufs=2))
         cpool = ctx.enter_context(tc.tile_pool(name="cpool", bufs=8))
         spool = ctx.enter_context(tc.tile_pool(name="spool", bufs=6))
-        opool = ctx.enter_context(tc.tile_pool(name="opool", bufs=3))
+        opool = ctx.enter_context(tc.tile_pool(name="opool", bufs=4))
         ps_t = ctx.enter_context(tc.psum_pool(name="ps_t", bufs=4))
         ps_o = ctx.enter_context(tc.psum_pool(name="ps_o", bufs=4))
         ctx.enter_context(tc.manual_schedule())
 
         ident = const.tile([P, P], F32, name="ident")
         make_identity(nc, ident[:])
+        ident_bf = const.tile([P, P], BF16, name="ident_bf")
+        make_identity(nc, ident_bf[:])
 
         x_tiles = {}
 
@@ -85,11 +88,14 @@ def tile_mymodel_t_kernel(tc, x_real, x_imag, w_real, w_imag, out):
             else:
                 nc.scalar.copy(out=o_ap, in_=i_ap)
 
-        def negate_w(oh, h):
+        def negate_w(oh, h, eng="v"):
             if ("n", oh) not in w_grouped:
                 w_grouped[("n", oh)] = wgpool.tile([P, 4096], BF16, name="g", align_bytes=64)
             cols = slice(h * 2048, (h + 1) * 2048)
-            nc.vector.tensor_scalar_mul(out=w_grouped[("n", oh)][:, cols], in0=w_grouped[("i", oh)][:, cols], scalar1=-1.0)
+            if eng == "s":
+                nc.scalar.mul(out=w_grouped[("n", oh)][:, cols], in_=w_grouped[("i", oh)][:, cols], mul=-1.0)
+            else:
+                nc.vector.tensor_scalar_mul(out=w_grouped[("n", oh)][:, cols], in0=w_grouped[("i", oh)][:, cols], scalar1=-1.0)
 
         def quant_w(v, oh, h):
             cols = slice(h * 512, (h + 1) * 512)
@@ -115,6 +121,23 @@ def tile_mymodel_t_kernel(tc, x_real, x_imag, w_real, w_imag, out):
 
         def turn(u, s):
             bt, h = u // 2, u % 2
+            if u in DIRECT:
+                xb = x_tiles[(bt, s)][:].rearrange("p (j t m) -> p t m j", t=4, m=NM)
+                for mpl in range(2):
+                    tb = ps_t.tile([P, 1024], BF16, name="tb")
+                    tv = tb[:].rearrange("p (m b t) -> p m b t", m=2, t=4)
+                    tw = tb[:].bitcast(F32).rearrange("p (m b w) -> p m b w", m=2, w=2)
+                    for mi in range(2):
+                        for t in (1, 0, 3, 2):
+                            nc.tensor.matmul(
+                                out=tw[:, mi, :, t // 2] if t % 2 == 1 else tv[:, mi, :, t],
+                                lhsT=xb[:, t, 4 * h + 2 * mpl + mi, :],
+                                rhs=ident_bf[:],
+                                start=True,
+                                stop=True,
+                            )
+                    x_banks[(u, s, mpl)] = tb
+                return
             xw = x_tiles[(bt, s)][:].bitcast(F32).rearrange("p (j t q) -> p t q j", t=4, q=4)
             if (u, s) in x_sorted:
                 xw = x_sorted[(u, s)][:].bitcast(F32).rearrange("p (m u j) -> p m u j", m=4, u=2)
@@ -136,7 +159,9 @@ def tile_mymodel_t_kernel(tc, x_real, x_imag, w_real, w_imag, out):
             bank = x_banks[(u, s, mpl)]
             o_ap = part.rearrange("p (m b t) -> p m b t", m=2, t=4)
             i_ap = bank[:].bitcast(BF16).rearrange("p (t b m) -> p m b t", t=4, m=2)
-            if (u, s) in x_sorted:
+            if u in DIRECT:
+                o_ap, i_ap = part.bitcast(F32), bank[:].bitcast(F32)
+            elif (u, s) in x_sorted:
                 o_ap = part.bitcast(F32).rearrange("p (m b u) -> p m b u", m=2, u=2)
                 i_ap = bank[:].rearrange("p (m u b) -> p m b u", m=2, u=2)
             if eng == "v":
@@ -194,7 +219,7 @@ def tile_mymodel_t_kernel(tc, x_real, x_imag, w_real, w_imag, out):
                         in_=ot[:].rearrange("p k o m -> p k (o m)"),
                     )
 
-        load_w("i", 0)
+        load_w("i", 0, 2)
         load_x(0)
         load_w("r", 0)
         load_x(1)
@@ -203,13 +228,14 @@ def tile_mymodel_t_kernel(tc, x_real, x_imag, w_real, w_imag, out):
         load_x(2)
         load_x(3)
 
-        regroup_w("v", "i", 0, 0)
-        regroup_w("s", "i", 0, 1)
+        for k in range(2):
+            regroup_w("v", "i", 0, 0, P // 2 * k, P // 2 * (k + 1))
+            regroup_w("s", "i", 0, 1, P // 2 * k, P // 2 * (k + 1))
         turn(0, 0)
         turn(1, 0)
         quant_w("i", 0, 0)
         negate_w(0, 0)
-        negate_w(0, 1)
+        negate_w(0, 1, "s")
         quant_w("i", 0, 1)
         quant_w("n", 0, 0)
         quant_w("n", 0, 1)
@@ -239,6 +265,7 @@ def tile_mymodel_t_kernel(tc, x_real, x_imag, w_real, w_imag, out):
         loaded = 4
         w2 = [("i", 0), ("n", 0), ("r", 0), ("i", 1), ("n", 1), ("r", 1)]
         w2_count = (0, 1, 2, 1, 2)
+        ns = len(steps)
 
         def goal(k, at):
             ahead = max(2 * (2 * b + hh) + 2 for b, o, hh in steps[: k + 2])
@@ -249,7 +276,9 @@ def tile_mymodel_t_kernel(tc, x_real, x_imag, w_real, w_imag, out):
                 load_x(loaded)
                 loaded += 1
             need = goal(k, done)
-            turn_to = goal(k + 1, need) if bt >= 2 and k % 2 == 0 else need
+            turn_to = need
+            if k % 2 == 0 and k >= 8:
+                turn_to = goal(k + 1, need)
             while turned < turn_to:
                 while sorted_to < 2 * NU and sorted_to <= turned + 2:
                     sort_x(sorted_to // 2, sorted_to % 2)
@@ -261,8 +290,6 @@ def tile_mymodel_t_kernel(tc, x_real, x_imag, w_real, w_imag, out):
                 drain(u, s, 0, "s")
                 drain(u, s, 1, "s")
                 done += 1
-                if done % 2 == 1 and done // 2 - 1 not in x_codes:
-                    quant_x(done // 2 - 1)
             for v, hh in w2[sum(w2_count[:k]) : sum(w2_count[: k + 1])]:
                 if v == "n":
                     negate_w(1, hh)
@@ -271,6 +298,6 @@ def tile_mymodel_t_kernel(tc, x_real, x_imag, w_real, w_imag, out):
                 quant_w(v, 1, hh)
             if 2 * bt + h not in x_codes:
                 quant_x(2 * bt + h)
-            mu(bt, banks, h, "sv" if h == 1 else "ss", k == len(steps) - 1)
+            mu(bt, banks, h, "sv" if k >= ns - 20 and k % 2 == 0 else "ss", k == ns - 1)
             if done // 2 - 1 not in x_codes and done % 2 == 0:
                 quant_x(done // 2 - 1)

@@ -125,12 +125,12 @@ def tile_mymodel_t_kernel(tc, x_real, x_imag, w_real, w_imag, out):
                 xb = x_tiles[(bt, s)][:].rearrange("p (j t m) -> p t m j", t=4, m=NM)
                 for mpl in range(2):
                     tb = ps_t.tile([P, 1024], BF16, name="tb")
-                    tv = tb[:].rearrange("p (m b t) -> p m b t", m=2, t=4)
-                    tw = tb[:].bitcast(F32).rearrange("p (m b w) -> p m b w", m=2, w=2)
+                    tv = tb[:].rearrange("p (m w b e) -> p m w b e", m=2, w=2, e=2)
+                    tw = tb[:].bitcast(F32).rearrange("p (m w b) -> p m w b", m=2, w=2)
                     for mi in range(2):
                         for t in (1, 0, 3, 2):
                             nc.tensor.matmul(
-                                out=tw[:, mi, :, t // 2] if t % 2 == 1 else tv[:, mi, :, t],
+                                out=tw[:, mi, t // 2, :] if t % 2 == 1 else tv[:, mi, t // 2, :, 0],
                                 lhsT=xb[:, t, 4 * h + 2 * mpl + mi, :],
                                 rhs=ident_bf[:],
                                 start=True,
@@ -160,7 +160,8 @@ def tile_mymodel_t_kernel(tc, x_real, x_imag, w_real, w_imag, out):
             o_ap = part.rearrange("p (m b t) -> p m b t", m=2, t=4)
             i_ap = bank[:].bitcast(BF16).rearrange("p (t b m) -> p m b t", t=4, m=2)
             if u in DIRECT:
-                o_ap, i_ap = part.bitcast(F32), bank[:].bitcast(F32)
+                o_ap = part.bitcast(F32).rearrange("p (m b u) -> p m b u", m=2, u=2)
+                i_ap = bank[:].bitcast(F32).rearrange("p (m u b) -> p m b u", m=2, u=2)
             elif (u, s) in x_sorted:
                 o_ap = part.bitcast(F32).rearrange("p (m b u) -> p m b u", m=2, u=2)
                 i_ap = bank[:].rearrange("p (m u b) -> p m b u", m=2, u=2)

from contextlib import ExitStack

import concourse.mybir as mybir
from concourse.masks import make_identity

F32 = mybir.dt.float32
BF16 = mybir.dt.bfloat16
U32 = mybir.dt.uint32
U8 = mybir.dt.uint8
FP8X4 = mybir.dt.float8_e4m3fn_x4

P = 128
B, I, O, NM = 1024, 512, 256, 8
NBT = B // P
NU = 2 * NBT
FIRST_SORTED = 6
DIRECT = (3, 5)
FLOPS = 2 * 4 * NM * B * I * O


def tile_mymodel_t_kernel(tc, x_real, x_imag, w_real, w_imag, out):
    nc = tc.nc
    xs_dram = [
        x_real.rearrange("b i x y z -> b (i x y z)"),
        x_imag.rearrange("b i x y z -> b (i x y z)"),
    ]
    w_dram = {
        "r": w_real.rearrange("(p t) o x y z -> p t (o x y z)", t=4),
        "i": w_imag.rearrange("(p t) o x y z -> p t (o x y z)", t=4),
    }
    out_dram = out.rearrange("c b o x y z -> b c (o x y z)")

    with ExitStack() as ctx:
        const = ctx.enter_context(tc.tile_pool(name="const", bufs=1))
        big = ctx.enter_context(tc.tile_pool(name="big", bufs=8))
        wpool = ctx.enter_context(tc.tile_pool(name="wpool", bufs=1))
        wgpool = ctx.enter_context(tc.tile_pool(name="wgpool", bufs=3))
        gpool = ctx.enter_context(tc.tile_pool(name="gpool", bufs=2))
        cpool = ctx.enter_context(tc.tile_pool(name="cpool", bufs=8))
        spool = ctx.enter_context(tc.tile_pool(name="spool", bufs=6))
        opool = ctx.enter_context(tc.tile_pool(name="opool", bufs=4))
        ps_t = ctx.enter_context(tc.psum_pool(name="ps_t", bufs=4))
        ps_o = ctx.enter_context(tc.psum_pool(name="ps_o", bufs=4))
        ctx.enter_context(tc.manual_schedule())

        ident = const.tile([P, P], F32, name="ident")
        make_identity(nc, ident[:])
        ident_bf = const.tile([P, P], BF16, name="ident_bf")
        make_identity(nc, ident_bf[:])

        x_tiles = {}

        def load_x(bt):
            for s in range(2):
                xt = big.tile([P, I * NM], BF16, name="xt", tag="big")
                nc.sync.dma_start(out=xt[:], in_=xs_dram[s][bt * P : (bt + 1) * P, :])
                x_tiles[(bt, s)] = xt

        w_raw = {}

        def load_w(v, oh, parts=1):
            wt = big.tile([P, 4, P * NM], BF16, name="wt", tag="big")
            width = P * NM // parts
            for k in range(parts):
                nc.sync.dma_start(
                    out=wt[:, :, k * width : (k + 1) * width],
                    in_=w_dram[v][:, :, oh * P * NM + k * width : oh * P * NM + (k + 1) * width],
                )
            w_raw[(v, oh)] = wt

        w_codes = {}
        w_scales = {}
        for v in ("r", "i", "n"):
            for oh in range(2):
                w_codes[(v, oh)] = wpool.tile([P, NM * P], U32, name="wc_%s%d" % (v, oh), align_bytes=64)
                w_scales[(v, oh)] = wpool.tile([P, NM * P], U8, name="ws_%s%d" % (v, oh), align_bytes=64)

        w_grouped = {}

        def regroup_w(eng, v, oh, h, o0=0, o1=P):
            if (v, oh) not in w_grouped:
                w_grouped[(v, oh)] = wgpool.tile([P, 4096], BF16, name="g", align_bytes=64)
            g = w_grouped[(v, oh)][:, h * 2048 : (h + 1) * 2048]
            o_ap = g.rearrange("p (m o t) -> p o t m", m=4, t=4)[:, o0:o1]
            i_ap = w_raw[(v, oh)][:].rearrange("p t (o m) -> p o t m", m=NM)[:, o0:o1, :, 4 * h : 4 * h + 4]
            if eng == "v":
                nc.vector.tensor_copy(out=o_ap, in_=i_ap)
            else:
                nc.scalar.copy(out=o_ap, in_=i_ap)

        def negate_w(oh, h, eng="v"):
            if ("n", oh) not in w_grouped:
                w_grouped[("n", oh)] = wgpool.tile([P, 4096], BF16, name="g", align_bytes=64)
            cols = slice(h * 2048, (h + 1) * 2048)
            if eng == "s":
                nc.scalar.mul(out=w_grouped[("n", oh)][:, cols], in_=w_grouped[("i", oh)][:, cols], mul=-1.0)
            else:
                nc.vector.tensor_scalar_mul(out=w_grouped[("n", oh)][:, cols], in0=w_grouped[("i", oh)][:, cols], scalar1=-1.0)

        def quant_w(v, oh, h):
            cols = slice(h * 512, (h + 1) * 512)
            nc.vector.quantize_mx(
                out=w_codes[(v, oh)][:, cols].bitcast(FP8X4),
                scales=w_scales[(v, oh)][:, cols],
                in_=w_grouped[(v, oh)][:, h * 2048 : (h + 1) * 2048],
            )

        x_sorted = {}

        def sort_x(u, s):
            bt, h = u // 2, u % 2
            xs = spool.tile([P, 4 * I], BF16, name="xs")
            o_ap = xs[:].rearrange("p (m u j e) -> p u j e m", m=4, u=2, e=2)
            i_ap = x_tiles[(bt, s)][:].rearrange("p (j u e m) -> p u j e m", u=2, e=2, m=NM)[:, :, :, :, 4 * h : 4 * h + 4]
            nc.vector.tensor_copy(out=o_ap, in_=i_ap)
            x_sorted[(u, s)] = xs

        x_codes = {}
        x_banks = {}
        x_grouped = {}

        def turn(u, s):
            bt, h = u // 2, u % 2
            if u in DIRECT:
                xb = x_tiles[(bt, s)][:].rearrange("p (j t m) -> p t m j", t=4, m=NM)
                for mpl in range(2):
                    tb = ps_t.tile([P, 1024], BF16, name="tb")
                    tv = tb[:].rearrange("p (m w b e) -> p m w b e", m=2, w=2, e=2)
                    tw = tb[:].bitcast(F32).rearrange("p (m w b) -> p m w b", m=2, w=2)
                    for mi in range(2):
                        for t in (1, 0, 3, 2):
                            nc.tensor.matmul(
                                out=tw[:, mi, t // 2, :] if t % 2 == 1 else tv[:, mi, t // 2, :, 0],
                                lhsT=xb[:, t, 4 * h + 2 * mpl + mi, :],
                                rhs=ident_bf[:],
                                start=True,
                                stop=True,
                            )
                    x_banks[(u, s, mpl)] = tb
                return
            xw = x_tiles[(bt, s)][:].bitcast(F32).rearrange("p (j t q) -> p t q j", t=4, q=4)
            if (u, s) in x_sorted:
                xw = x_sorted[(u, s)][:].bitcast(F32).rearrange("p (m u j) -> p m u j", m=4, u=2)
            for mpl in range(2):
                tb = ps_t.tile([P, 512], F32, name="tb")
                for t in range(4):
                    if (u, s) in x_sorted:
                        src = xw[:, 2 * mpl + t // 2, t % 2, :]
                    else:
                        src = xw[:, t, 2 * h + mpl, :]
                    nc.tensor.transpose(tb[:, t * P : (t + 1) * P], src, ident[:])
                x_banks[(u, s, mpl)] = tb

        def drain(u, s, mpl, eng):
            if u not in x_grouped:
                x_grouped[u] = gpool.tile([P, 4096], BF16, name="grouped", align_bytes=64)
            k = 2 * s + mpl
            part = x_grouped[u][:, k * 1024 : (k + 1) * 1024]
            bank = x_banks[(u, s, mpl)]
            o_ap = part.rearrange("p (m b t) -> p m b t", m=2, t=4)
            i_ap = bank[:].bitcast(BF16).rearrange("p (t b m) -> p m b t", t=4, m=2)
            if u in DIRECT:
                o_ap = part.bitcast(F32).rearrange("p (m b u) -> p m b u", m=2, u=2)
                i_ap = bank[:].bitcast(F32).rearrange("p (m u b) -> p m b u", m=2, u=2)
            elif (u, s) in x_sorted:
                o_ap = part.bitcast(F32).rearrange("p (m b u) -> p m b u", m=2, u=2)
                i_ap = bank[:].rearrange("p (m u b) -> p m b u", m=2, u=2)
            if eng == "v":
                nc.vector.tensor_copy(out=o_ap, in_=i_ap)
            else:
                nc.scalar.copy(out=o_ap, in_=i_ap)

        def quant_x(u):
            xc = cpool.tile([P, 1024], U32, name="xc", align_bytes=64)
            xsc = cpool.tile([P, 1024], U8, name="xsc", align_bytes=64)
            nc.vector.quantize_mx(out=xc[:].bitcast(FP8X4), scales=xsc[:], in_=x_grouped[u][:])
            x_codes[u] = (xc, xsc)

        out_tiles = {}

        def out_piece(bt, c, oh):
            return out_dram[bt * P : (bt + 1) * P, c, oh * P * NM : (oh + 1) * P * NM]

        def mu(bt, banks, h, engs, last):
            if h == 0:
                out_tiles[(bt, banks)] = opool.tile([P, 2, P, NM], F32, name="ot")
            ot = out_tiles[(bt, banks)]
            xc, xsc = x_codes[2 * bt + h]
            for k, (c, oh) in enumerate(banks):
                ob = ps_o.tile([P, 512], F32, name="ob")
                for ml in range(4):
                    pairs = ((0, "r"), (1, "n")) if c == 0 else ((0, "i"), (1, "r"))
                    for n, (s, v) in enumerate(pairs):
                        sl = slice((4 * s + ml) * P, (4 * s + ml + 1) * P)
                        wl = slice((4 * h + ml) * P, (4 * h + ml + 1) * P)
                        nc.tensor.matmul_mx(
                            out=ob[:, ml * P : (ml + 1) * P],
                            lhsT=xc[:, sl].bitcast(FP8X4),
                            lhsT_scale=xsc[:, sl],
                            rhs=w_codes[(v, oh)][:, wl].bitcast(FP8X4),
                            rhs_scale=w_scales[(v, oh)][:, wl],
                            start=(n == 0),
                            stop=(n == 1),
                        )
                o_ap = ot[:, k, :, 4 * h : 4 * h + 4]
                i_ap = ob[:].rearrange("p (m o) -> p o m", m=4)
                if engs[k] == "v":
                    nc.vector.tensor_copy(out=o_ap, in_=i_ap)
                else:
                    nc.scalar.copy(out=o_ap, in_=i_ap)
                if last and h == 1:
                    nc.sync.dma_start(out=out_piece(bt, c, oh), in_=ot[:, k].rearrange("p o m -> p (o m)"))
            if h == 1 and not last:
                (c0, h0), (c1, h1) = banks
                if c0 == c1:
                    nc.sync.dma_start(out=out_dram[bt * P : (bt + 1) * P, c0, :], in_=ot[:].rearrange("p k o m -> p (k o m)"))
                else:
                    nc.sync.dma_start(
                        out=out_dram[bt * P : (bt + 1) * P, :, h0 * P * NM : (h0 + 1) * P * NM],
                        in_=ot[:].rearrange("p k o m -> p k (o m)"),
                    )

        load_w("i", 0, 2)
        load_x(0)
        load_w("r", 0)
        load_x(1)
        load_w("i", 1)
        load_w("r", 1)
        load_x(2)
        load_x(3)

        for k in range(2):
            regroup_w("v", "i", 0, 0, P // 2 * k, P // 2 * (k + 1))
            regroup_w("s", "i", 0, 1, P // 2 * k, P // 2 * (k + 1))
        turn(0, 0)
        turn(1, 0)
        quant_w("i", 0, 0)
        negate_w(0, 0)
        negate_w(0, 1, "s")
        quant_w("i", 0, 1)
        quant_w("n", 0, 0)
        quant_w("n", 0, 1)
        drain(0, 0, 0, "s")
        drain(0, 0, 1, "s")
        turn(0, 1)
        drain(1, 0, 0, "v")
        drain(1, 0, 1, "s")
        turn(1, 1)
        drain(0, 1, 0, "v")
        drain(0, 1, 1, "s")
        regroup_w("v", "r", 0, 0)
        quant_x(0)
        drain(1, 1, 0, "s")
        drain(1, 1, 1, "s")
        quant_w("r", 0, 0)
        regroup_w("v", "r", 0, 1)
        quant_x(1)
        quant_w("r", 0, 1)

        mus = [(bt, ((0, oh), (1, oh))) for oh in range(2) for bt in range(2)]
        mus += [(bt, ((c, 0), (c, 1))) for bt in range(2, NBT) for c in range(2)]
        steps = [(bt, banks, h) for bt, banks in mus for h in range(2)]
        done = 4
        turned = 4
        sorted_to = 2 * FIRST_SORTED
        loaded = 4
        w2 = [("i", 0), ("n", 0), ("r", 0), ("i", 1), ("n", 1), ("r", 1)]
        w2_count = (0, 1, 2, 1, 2)
        ns = len(steps)

        def goal(k, at):
            ahead = max(2 * (2 * b + hh) + 2 for b, o, hh in steps[: k + 2])
            return min(2 * NU, max(ahead, at + 1))

        for k, (bt, banks, h) in enumerate(steps):
            while loaded < NBT and loaded <= done // 4 + 2:
                load_x(loaded)
                loaded += 1
            need = goal(k, done)
            turn_to = need
            if k % 2 == 0 and k >= 8:
                turn_to = goal(k + 1, need)
            while turned < turn_to:
                while sorted_to < 2 * NU and sorted_to <= turned + 2:
                    sort_x(sorted_to // 2, sorted_to % 2)
                    sorted_to += 1
                turn(turned // 2, turned % 2)
                turned += 1
            while done < need:
                u, s = done // 2, done % 2
                drain(u, s, 0, "s")
                drain(u, s, 1, "s")
                done += 1
            for v, hh in w2[sum(w2_count[:k]) : sum(w2_count[: k + 1])]:
                if v == "n":
                    negate_w(1, hh)
                else:
                    regroup_w("v", v, 1, hh)
                quant_w(v, 1, hh)
            if 2 * bt + h not in x_codes:
                quant_x(2 * bt + h)
            mu(bt, banks, h, "sv" if k >= ns - 20 and k % 2 == 0 else "ss", k == ns - 1)
            if done // 2 - 1 not in x_codes and done % 2 == 0:
                quant_x(done // 2 - 1)
